import numpy as np
import ml_dtypes


def mxq(x, axis, fmt="e4m3"):
    dtype, down = {"e4m3": (ml_dtypes.float8_e4m3fn, 7), "e5m2": (ml_dtypes.float8_e5m2, 14)}[fmt]
    v = np.moveaxis(np.asarray(x, np.float32).astype(ml_dtypes.bfloat16).astype(np.float64), axis, -1)
    blocks = v.reshape(v.shape[:-1] + (-1, 32))
    amax = np.abs(blocks).max(-1, keepdims=True)
    byte = np.maximum(np.where(amax > 0, np.frexp(amax)[1] - 1 + 127, 0) - down, 1)
    scale = np.exp2(byte - 127.0)
    codes = (blocks / scale).astype(np.float32).astype(dtype).astype(np.float64)
    return np.moveaxis((codes * scale).reshape(v.shape), -1, axis)


WIDE = False


def mx_kscale(k):
    if not WIDE:
        return np.ones(k)
    levels = np.array([10, -10, 5, -5, 0])
    a = np.random.permutation(np.resize(levels, k // 512 * 4)).reshape(k // 512, 4)
    idx = np.arange(k)
    return np.exp2(a[idx // 512, idx % 128 // 32])


BF16 = ml_dtypes.bfloat16


def bf(x):
    return np.asarray(x, np.float32).astype(BF16)


def f64(x):
    return np.asarray(x).astype(np.float64)


B, T, C, H, NOPE, ROPE, VD, LORA = 1, 512, 2048, 16, 128, 128, 128, 512
EPS = 1e-6
HALF = ROPE // 2
KVW = H * (NOPE + VD)


def make_freq_cis():
    inv = 1.0 / (10000.0 ** (np.arange(0, ROPE, 2) / ROPE))
    ang = np.outer(np.arange(T), inv)
    return np.stack([np.cos(ang), np.sin(ang)], -1)


def apply_rope(v, fc):
    vr = v.reshape(B, T, HALF, 2)
    real = vr[..., 0] * fc[..., 0] - vr[..., 1] * fc[..., 1]
    imag = vr[..., 1] * fc[..., 0] + vr[..., 0] * fc[..., 1]
    return np.stack([real, imag], -1).reshape(B, T, ROPE)


def setup_inputs():
    s, t = mx_kscale(C), mx_kscale(LORA)
    return {"x": bf(np.random.standard_normal((B, T, C)) * s),
            "freq_cis": bf(make_freq_cis()),
            "Wckv": bf(np.random.standard_normal((C, LORA + ROPE)) / np.sqrt(C) / s[:, None]),
            "kv_norm_w": bf((1.0 + 0.1 * np.random.standard_normal(LORA)) * t),
            "Wdkv": bf(np.random.standard_normal((LORA, KVW)) / np.sqrt(LORA) / t[:, None])}


def reference(x, freq_cis, Wckv, kv_norm_w, Wdkv):
    ckv = mxq(f64(x), 2, "e4m3") @ mxq(f64(Wckv), 0, "e4m3")
    kv_lat, k_rope = ckv[..., :LORA], ckv[..., LORA:]
    k_rope = apply_rope(k_rope, f64(freq_cis))
    lat_n = kv_lat / np.sqrt(np.mean(kv_lat * kv_lat, -1, keepdims=True) + EPS) * f64(kv_norm_w)
    kv = mxq(lat_n, 2, "e4m3") @ mxq(f64(Wdkv), 0, "e4m3")
    return kv, k_rope

@@ -1,0 +1,243 @@
+from contextlib import ExitStack
+
+import concourse.mybir as mybir
+from concourse.masks import make_identity
+
+F32 = mybir.dt.float32
+BF16 = mybir.dt.bfloat16
+U32 = mybir.dt.uint32
+U8 = mybir.dt.uint8
+FP8X4 = mybir.dt.float8_e4m3fn_x4
+ACT = mybir.ActivationFunctionType
+ALU = mybir.AluOpType
+
+P = 128
+PACK = 4
+K_PASS = P * PACK
+
+T = 512
+C = 2048
+LORA = 512
+ROPE = 128
+KVW = 4096
+EPS = 1e-6
+
+TOK_TILES = T // P
+PASSES = C // K_PASS
+N_TILE = 512
+W2_LOAD = 1024
+W2_LOADS = KVW // W2_LOAD
+HALVES = W2_LOAD // N_TILE
+W1_VECTOR_COLS = 384
+
+FLOPS = 2 * T * C * (LORA + ROPE) + 2 * T * LORA * KVW
+
+
+def regroup(copy, grouped, raw):
+    copy(
+        out=grouped.rearrange("p (c i) t -> p c t i", i=4),
+        in_=raw.rearrange("p t (c i) -> p c t i", i=4),
+    )
+
+
+def tile_multiheadlatentattention_pa_kernel(tc, x, freq_cis, Wckv, kv_norm_w, Wdkv, out_0, out_1):
+    nc = tc.nc
+    x_rows = x.flatten_outer_dims()
+    kv_rows = out_0.flatten_outer_dims()
+    rope_rows = out_1.flatten_outer_dims()
+
+    with ExitStack() as ctx:
+        keep = ctx.enter_context(tc.tile_pool(name="keep", bufs=1))
+        work = ctx.enter_context(tc.tile_pool(name="work", bufs=2))
+        w2_work = ctx.enter_context(tc.tile_pool(name="w2_work", bufs=3))
+        store = ctx.enter_context(tc.tile_pool(name="store", bufs=6))
+        banks = ctx.enter_context(tc.psum_pool(name="banks", bufs=6))
+        fixed_banks = ctx.enter_context(tc.psum_pool(name="fixed_banks", bufs=1))
+
+        ident_f32 = keep.tile([P, P], F32, name="ident_f32")
+        make_identity(nc, ident_f32[:])
+        ident_bf16 = keep.tile([P, P], BF16, name="ident_bf16")
+        make_identity(nc, ident_bf16[:])
+        ones = keep.tile([P, P], BF16, name="ones")
+        nc.vector.memset(ones[:], 1.0)
+        eps = keep.tile([P, 1], F32, name="eps")
+        nc.vector.memset(eps[:], EPS)
+        warm = keep.tile([P, 1], F32, name="warm")
+        nc.scalar.activation(out=warm[:], in_=eps[:], func=ACT.Sqrt)
+
+        gain_row = keep.tile([P, LORA], BF16, name="gain_row")
+        nc.vector.memset(gain_row[:], 0.0)
+        nc.scalar.dma_start(out=gain_row[0:1, :], in_=kv_norm_w.rearrange("(o n) -> o n", o=1))
+
+        w1_raw = []
+        for g in range(PASSES):
+            raw = keep.tile([P, PACK, LORA + ROPE], BF16, name="w1_raw%d" % g)
+            nc.sync.dma_start(
+                out=raw[:].rearrange("q (u e) c -> q u (e c)", u=2),
+                in_=Wckv[g * K_PASS : (g + 1) * K_PASS, :].rearrange("(u q e) c -> q u (e c)", u=2, e=2),
+            )
+            w1_raw.append(raw)
+        x_raw = []
+        for m in range(TOK_TILES):
+            raw = keep.tile([P, C], BF16, name="x_raw%d" % m)
+            nc.sync.dma_start(out=raw[:], in_=x_rows[m * P : (m + 1) * P, :])
+            x_raw.append(raw)
+        w2_raw = []
+        for c in range(W2_LOADS):
+            raw = keep.tile([P, PACK, W2_LOAD], BF16, name="w2_raw%d" % c)
+            nc.sync.dma_start(
+                out=raw[:],
+                in_=Wdkv[:, c * W2_LOAD : (c + 1) * W2_LOAD].rearrange("(t p) n -> p t n", p=P),
+            )
+            w2_raw.append(raw)
+        freq = keep.tile([P, TOK_TILES, ROPE], BF16, name="freq")
+        nc.sync.dma_start(out=freq[:], in_=freq_cis.rearrange("(m p) i e -> p m (i e)", p=P))
+
+        gain_ps = banks.tile([P, N_TILE], F32, tag="bank", name="gain_ps")
+        nc.tensor.matmul(out=gain_ps[:], lhsT=ones[:], rhs=gain_row[:], start=True, stop=True)
+        gain = keep.tile([P, LORA], F32, name="gain")
+        nc.scalar.copy(out=gain[:], in_=gain_ps[:])
+
+        w1_lat_codes, w1_lat_scales, w1_rope_codes, w1_rope_scales = [], [], [], []
+        for g in range(PASSES):
+            lat_grouped = work.tile([P, LORA, PACK], BF16, tag="w1_lat_grouped", name="lat_grouped", align_bytes=64)
+            rope_grouped = work.tile([P, ROPE, PACK], BF16, tag="w1_rope_grouped", name="rope_grouped", align_bytes=64)
+            regroup(nc.vector.tensor_copy, lat_grouped[:, 0:W1_VECTOR_COLS, :], w1_raw[g][:, :, 0:W1_VECTOR_COLS])
+            regroup(nc.scalar.copy, lat_grouped[:, W1_VECTOR_COLS:LORA, :], w1_raw[g][:, :, W1_VECTOR_COLS:LORA])
+            regroup(nc.scalar.copy, rope_grouped[:], w1_raw[g][:, :, LORA : LORA + ROPE])
+            lat_codes = keep.tile([P, LORA], U32, name="w1_lat_codes%d" % g, align_bytes=64)
+            lat_scales = keep.tile([P, LORA], U8, name="w1_lat_scales%d" % g, align_bytes=64)
+            nc.vector.quantize_mx(
+                out=lat_codes[:].bitcast(FP8X4),
+                scales=lat_scales[:],
+                in_=lat_grouped[:].rearrange("p c t -> p (c t)"),
+            )
+            rope_codes = keep.tile([P, ROPE], U32, name="w1_rope_codes%d" % g, align_bytes=64)
+            rope_scales = keep.tile([P, ROPE], U8, name="w1_rope_scales%d" % g, align_bytes=64)
+            nc.vector.quantize_mx(
+                out=rope_codes[:].bitcast(FP8X4),
+                scales=rope_scales[:],
+                in_=rope_grouped[:].rearrange("p c t -> p (c t)"),
+            )
+            w1_lat_codes.append(lat_codes)
+            w1_lat_scales.append(lat_scales)
+            w1_rope_codes.append(rope_codes)
+            w1_rope_scales.append(rope_scales)
+
+        x_codes, x_scales = [], []
+        for m in range(TOK_TILES):
+            x_words = x_raw[m][:].bitcast(F32)
+            x_grouped = work.tile([P, PASSES, P, PACK], BF16, tag="x_grouped", name="x_grouped", align_bytes=64)
+            x_grouped_words = x_grouped[:].bitcast(F32)
+            for h in range(2):
+                xt = banks.tile([P, N_TILE], F32, tag="bank", name="xt")
+                for s in range(4):
+                    w0 = (4 * h + s) * P
+                    nc.tensor.transpose(xt[:, s * P : (s + 1) * P], x_words[:, w0 : w0 + P], ident_f32[:])
+                nc.scalar.copy(
+                    out=x_grouped_words[:, 2 * h : 2 * h + 2, :, :],
+                    in_=xt[:].rearrange("p (g u r) -> p g r u", g=2, u=2),
+                )
+            codes = keep.tile([P, PASSES, P], U32, name="x_codes%d" % m, align_bytes=64)
+            scales = keep.tile([P, PASSES, P], U8, name="x_scales%d" % m, align_bytes=64)
+            nc.vector.quantize_mx(
+                out=codes[:].rearrange("p g r -> p (g r)").bitcast(FP8X4),
+                scales=scales[:].rearrange("p g r -> p (g r)"),
+                in_=x_grouped[:].rearrange("p g r t -> p (g r t)"),
+            )
+            x_codes.append(codes)
+            x_scales.append(scales)
+
+        rope_ps = fixed_banks.tile([P, TOK_TILES, ROPE], F32, name="rope_ps")
+        n_codes, n_scales = [], []
+        for m in range(TOK_TILES):
+            lat_ps = banks.tile([P, N_TILE], F32, tag="bank", name="lat_ps")
+            for g in range(PASSES):
+                nc.tensor.matmul_mx(
+                    out=lat_ps[:],
+                    lhsT=x_codes[m][:, g, :].bitcast(FP8X4),
+                    lhsT_scale=x_scales[m][:, g, :],
+                    rhs=w1_lat_codes[g][:].bitcast(FP8X4),
+                    rhs_scale=w1_lat_scales[g][:],
+                    start=(g == 0),
+                    stop=(g == PASSES - 1),
+                )
+            for g in range(PASSES):
+                nc.tensor.matmul_mx(
+                    out=rope_ps[:, m, :],
+                    lhsT=x_codes[m][:, g, :].bitcast(FP8X4),
+                    lhsT_scale=x_scales[m][:, g, :],
+                    rhs=w1_rope_codes[g][:].bitcast(FP8X4),
+                    rhs_scale=w1_rope_scales[g][:],
+                    start=(g == 0),
+                    stop=(g == PASSES - 1),
+                )
+            squares = work.tile([P, LORA], F32, tag="squares", name="squares")
+            sum_sq = work.tile([P, 1], F32, tag="sum_sq", name="sum_sq")
+            nc.scalar.activation(out=squares[:], in_=lat_ps[:], func=ACT.Square, accum_out=sum_sq[:])
+            rms = work.tile([P, 1], F32, tag="rms", name="rms")
+            nc.scalar.activation(out=rms[:], in_=sum_sq[:], func=ACT.Sqrt, scale=1.0 / LORA, bias=eps[:])
+            inv_rms = work.tile([P, 1], F32, tag="inv_rms", name="inv_rms")
+            nc.vector.reciprocal(out=inv_rms[:], in_=rms[:])
+            n_bf16 = work.tile([P, LORA], BF16, tag="n_bf16", name="n_bf16")
+            nc.vector.scalar_tensor_tensor(
+                out=n_bf16[:], in0=lat_ps[:], scalar=inv_rms[:], in1=gain[:], op0=ALU.mult, op1=ALU.mult
+            )
+            n_t = fixed_banks.tile([P, PACK, P], BF16, name="n_t")
+            for t in range(PACK):
+                nc.tensor.transpose(n_t[:, t, :], n_bf16[:, t * P : (t + 1) * P], ident_bf16[:])
+            n_grouped = work.tile([P, P, PACK], BF16, tag="n_grouped", name="n_grouped", align_bytes=64)
+            nc.scalar.copy(out=n_grouped[:], in_=n_t[:].rearrange("p t r -> p r t"))
+            codes = keep.tile([P, P], U32, name="n_codes%d" % m, align_bytes=64)
+            scales = keep.tile([P, P], U8, name="n_scales%d" % m, align_bytes=64)
+            nc.vector.quantize_mx(
+                out=codes[:].bitcast(FP8X4), scales=scales[:], in_=n_grouped[:].rearrange("p r t -> p (r t)")
+            )
+            n_codes.append(codes)
+            n_scales.append(scales)
+
+        for c in range(W2_LOADS):
+            w2_codes, w2_scales = [], []
+            for h in range(HALVES):
+                cols = slice(h * N_TILE, (h + 1) * N_TILE)
+                w2_grouped = w2_work.tile([P, N_TILE, PACK], BF16, tag="w2_grouped", name="w2_grouped", align_bytes=64)
+                regroup(nc.vector.tensor_copy, w2_grouped[:], w2_raw[c][:, :, cols])
+                codes = keep.tile([P, N_TILE], U32, name="w2_codes%d_%d" % (c, h), align_bytes=64)
+                scales = keep.tile([P, N_TILE], U8, name="w2_scales%d_%d" % (c, h), align_bytes=64)
+                nc.vector.quantize_mx(
+                    out=codes[:].bitcast(FP8X4), scales=scales[:], in_=w2_grouped[:].rearrange("p c t -> p (c t)")
+                )
+                w2_codes.append(codes)
+                w2_scales.append(scales)
+            for m in range(TOK_TILES):
+                kv_sb = store.tile([P, W2_LOAD], F32, tag="kv_sb", name="kv_sb")
+                for h in range(HALVES):
+                    kv_ps = banks.tile([P, N_TILE], F32, tag="bank", name="kv_ps")
+                    nc.tensor.matmul_mx(
+                        out=kv_ps[:],
+                        lhsT=n_codes[m][:].bitcast(FP8X4),
+                        lhsT_scale=n_scales[m][:],
+                        rhs=w2_codes[h][:].bitcast(FP8X4),
+                        rhs_scale=w2_scales[h][:],
+                        start=True,
+                        stop=True,
+                    )
+                    nc.scalar.copy(out=kv_sb[:, h * N_TILE : (h + 1) * N_TILE], in_=kv_ps[:])
+                nc.sync.dma_start(
+                    out=kv_rows[m * P : (m + 1) * P, c * W2_LOAD : (c + 1) * W2_LOAD], in_=kv_sb[:]
+                )
+
+        pairs = TOK_TILES * ROPE // 2
+        kr = rope_ps[:].rearrange("p m (i e) -> p (m i) e", e=2)
+        table = freq[:].rearrange("p m (i e) -> p (m i) e", e=2)
+        by_cos = keep.tile([P, pairs, 2], F32, name="by_cos")
+        by_sin = keep.tile([P, pairs, 2], F32, name="by_sin")
+        rotated = keep.tile([P, pairs, 2], F32, name="rotated")
+        nc.vector.tensor_tensor(out=by_cos[:], in0=kr, in1=table[:, :, 0:1].to_broadcast([P, pairs, 2]), op=ALU.mult)
+        nc.vector.tensor_tensor(out=by_sin[:], in0=kr, in1=table[:, :, 1:2].to_broadcast([P, pairs, 2]), op=ALU.mult)
+        nc.vector.tensor_tensor(out=rotated[:, :, 0], in0=by_cos[:, :, 0], in1=by_sin[:, :, 1], op=ALU.subtract)
+        nc.vector.tensor_tensor(out=rotated[:, :, 1], in0=by_cos[:, :, 1], in1=by_sin[:, :, 0], op=ALU.add)
+        nc.sync.dma_start(
+            out=rope_rows.rearrange("(m p) f -> p m f", p=P),
+            in_=rotated[:].rearrange("p (m i) e -> p m (i e)", m=TOK_TILES),
+        )

@@ -28,7 +28,8 @@ N_TILE = 512
 W2_LOAD = 1024
 W2_LOADS = KVW // W2_LOAD
 HALVES = W2_LOAD // N_TILE
-W1_VECTOR_COLS = 384
+PIECES = KVW // N_TILE
+W1_VECTOR_COLS = 256
 
 FLOPS = 2 * T * C * (LORA + ROPE) + 2 * T * LORA * KVW
 
@@ -48,12 +49,14 @@ def tile_multiheadlatentattention_pa_kernel(tc, x, freq_cis, Wckv, kv_norm_w, Wd
 
     with ExitStack() as ctx:
         keep = ctx.enter_context(tc.tile_pool(name="keep", bufs=1))
-        work = ctx.enter_context(tc.tile_pool(name="work", bufs=2))
-        w2_work = ctx.enter_context(tc.tile_pool(name="w2_work", bufs=3))
-        store = ctx.enter_context(tc.tile_pool(name="store", bufs=6))
-        banks = ctx.enter_context(tc.psum_pool(name="banks", bufs=6))
+        work = ctx.enter_context(tc.tile_pool(name="work", bufs=3))
+        store = ctx.enter_context(tc.tile_pool(name="store", bufs=8))
+        banks = ctx.enter_context(tc.psum_pool(name="banks", bufs=7))
         fixed_banks = ctx.enter_context(tc.psum_pool(name="fixed_banks", bufs=1))
+        ctx.enter_context(tc.manual_schedule())
 
+        gain_row = keep.tile([P, LORA], BF16, name="gain_row")
+        nc.gpsimd.memset(gain_row[:], 0.0)
         ident_f32 = keep.tile([P, P], F32, name="ident_f32")
         make_identity(nc, ident_f32[:])
         ident_bf16 = keep.tile([P, P], BF16, name="ident_bf16")
@@ -65,31 +68,43 @@ def tile_multiheadlatentattention_pa_kernel(tc, x, freq_cis, Wckv, kv_norm_w, Wd
         warm = keep.tile([P, 1], F32, name="warm")
         nc.scalar.activation(out=warm[:], in_=eps[:], func=ACT.Sqrt)
 
-        gain_row = keep.tile([P, LORA], BF16, name="gain_row")
-        nc.vector.memset(gain_row[:], 0.0)
-        nc.scalar.dma_start(out=gain_row[0:1, :], in_=kv_norm_w.rearrange("(o n) -> o n", o=1))
+        nc.sync.dma_start(out=gain_row[0:1, :], in_=kv_norm_w.rearrange("(o n) -> o n", o=1))
 
-        w1_raw = []
-        for g in range(PASSES):
+        w1_raw, x_raw, w2_raw = {}, {}, {}
+
+        def load_w1(g):
             raw = keep.tile([P, PACK, LORA + ROPE], BF16, name="w1_raw%d" % g)
             nc.sync.dma_start(
                 out=raw[:].rearrange("q (u e) c -> q u (e c)", u=2),
                 in_=Wckv[g * K_PASS : (g + 1) * K_PASS, :].rearrange("(u q e) c -> q u (e c)", u=2, e=2),
             )
-            w1_raw.append(raw)
-        x_raw = []
-        for m in range(TOK_TILES):
+            w1_raw[g] = raw
+
+        def load_x(m):
             raw = keep.tile([P, C], BF16, name="x_raw%d" % m)
             nc.sync.dma_start(out=raw[:], in_=x_rows[m * P : (m + 1) * P, :])
-            x_raw.append(raw)
-        w2_raw = []
-        for c in range(W2_LOADS):
+            x_raw[m] = raw
+
+        def load_w2(c):
             raw = keep.tile([P, PACK, W2_LOAD], BF16, name="w2_raw%d" % c)
             nc.sync.dma_start(
                 out=raw[:],
                 in_=Wdkv[:, c * W2_LOAD : (c + 1) * W2_LOAD].rearrange("(t p) n -> p t n", p=P),
             )
-            w2_raw.append(raw)
+            w2_raw[c] = raw
+
+        load_w1(0)
+        load_w1(1)
+        load_w1(2)
+        load_w1(3)
+        load_x(0)
+        load_x(1)
+        load_x(2)
+        load_x(3)
+        load_w2(0)
+        load_w2(1)
+        load_w2(2)
+        load_w2(3)
         freq = keep.tile([P, TOK_TILES, ROPE], BF16, name="freq")
         nc.sync.dma_start(out=freq[:], in_=freq_cis.rearrange("(m p) i e -> p m (i e)", p=P))
 
@@ -98,146 +113,266 @@ def tile_multiheadlatentattention_pa_kernel(tc, x, freq_cis, Wckv, kv_norm_w, Wd
         gain = keep.tile([P, LORA], F32, name="gain")
         nc.scalar.copy(out=gain[:], in_=gain_ps[:])
 
-        w1_lat_codes, w1_lat_scales, w1_rope_codes, w1_rope_scales = [], [], [], []
-        for g in range(PASSES):
-            lat_grouped = work.tile([P, LORA, PACK], BF16, tag="w1_lat_grouped", name="lat_grouped", align_bytes=64)
-            rope_grouped = work.tile([P, ROPE, PACK], BF16, tag="w1_rope_grouped", name="rope_grouped", align_bytes=64)
-            regroup(nc.vector.tensor_copy, lat_grouped[:, 0:W1_VECTOR_COLS, :], w1_raw[g][:, :, 0:W1_VECTOR_COLS])
-            regroup(nc.scalar.copy, lat_grouped[:, W1_VECTOR_COLS:LORA, :], w1_raw[g][:, :, W1_VECTOR_COLS:LORA])
-            regroup(nc.scalar.copy, rope_grouped[:], w1_raw[g][:, :, LORA : LORA + ROPE])
-            lat_codes = keep.tile([P, LORA], U32, name="w1_lat_codes%d" % g, align_bytes=64)
-            lat_scales = keep.tile([P, LORA], U8, name="w1_lat_scales%d" % g, align_bytes=64)
-            nc.vector.quantize_mx(
-                out=lat_codes[:].bitcast(FP8X4),
-                scales=lat_scales[:],
-                in_=lat_grouped[:].rearrange("p c t -> p (c t)"),
-            )
-            rope_codes = keep.tile([P, ROPE], U32, name="w1_rope_codes%d" % g, align_bytes=64)
-            rope_scales = keep.tile([P, ROPE], U8, name="w1_rope_scales%d" % g, align_bytes=64)
-            nc.vector.quantize_mx(
-                out=rope_codes[:].bitcast(FP8X4),
-                scales=rope_scales[:],
-                in_=rope_grouped[:].rearrange("p c t -> p (c t)"),
-            )
-            w1_lat_codes.append(lat_codes)
-            w1_lat_scales.append(lat_scales)
-            w1_rope_codes.append(rope_codes)
-            w1_rope_scales.append(rope_scales)
+        w1_grouped, w1_codes, w1_scales = {}, {}, {}
+        rope_grouped = keep.tile([P, PASSES, ROPE, PACK], BF16, name="rope_grouped", align_bytes=64)
+        rope_codes = keep.tile([P, PASSES, ROPE], U32, name="rope_codes", align_bytes=64)
+        rope_scales = keep.tile([P, PASSES, ROPE], U8, name="rope_scales", align_bytes=64)
 
-        x_codes, x_scales = [], []
-        for m in range(TOK_TILES):
+        def w1_regroup(g):
+            grouped = work.tile([P, LORA, PACK], BF16, tag="w1_grouped", name="w1_grouped", align_bytes=64)
+            regroup(nc.vector.tensor_copy, grouped[:, 0:W1_VECTOR_COLS, :], w1_raw[g][:, :, 0:W1_VECTOR_COLS])
+            regroup(nc.scalar.copy, grouped[:, W1_VECTOR_COLS:LORA, :], w1_raw[g][:, :, W1_VECTOR_COLS:LORA])
+            w1_grouped[g] = grouped
+
+        def rope_regroup(g):
+            regroup(nc.vector.tensor_copy, rope_grouped[:, g, :, :], w1_raw[g][:, :, LORA : LORA + ROPE])
+
+        def w1_quantise(g):
+            codes = keep.tile([P, LORA], U32, name="w1_codes%d" % g, align_bytes=64)
+            scales = keep.tile([P, LORA], U8, name="w1_scales%d" % g, align_bytes=64)
+            nc.vector.quantize_mx(
+                out=codes[:].bitcast(FP8X4), scales=scales[:], in_=w1_grouped[g][:].rearrange("p c t -> p (c t)")
+            )
+            w1_codes[g] = codes
+            w1_scales[g] = scales
+
+        def rope_quantise():
+            nc.vector.quantize_mx(
+                out=rope_codes[:].rearrange("p g c -> p (g c)").bitcast(FP8X4),
+                scales=rope_scales[:].rearrange("p g c -> p (g c)"),
+                in_=rope_grouped[:].rearrange("p g c t -> p (g c t)"),
+            )
+
+        x_banks, x_grouped, x_codes, x_scales = {}, {}, {}, {}
+
+        def x_transpose(m):
             x_words = x_raw[m][:].bitcast(F32)
-            x_grouped = work.tile([P, PASSES, P, PACK], BF16, tag="x_grouped", name="x_grouped", align_bytes=64)
-            x_grouped_words = x_grouped[:].bitcast(F32)
+            x_banks[m] = []
             for h in range(2):
                 xt = banks.tile([P, N_TILE], F32, tag="bank", name="xt")
                 for s in range(4):
                     w0 = (4 * h + s) * P
                     nc.tensor.transpose(xt[:, s * P : (s + 1) * P], x_words[:, w0 : w0 + P], ident_f32[:])
-                nc.scalar.copy(
-                    out=x_grouped_words[:, 2 * h : 2 * h + 2, :, :],
-                    in_=xt[:].rearrange("p (g u r) -> p g r u", g=2, u=2),
+                x_banks[m].append(xt)
+
+        def x_copy(m, copies=(nc.scalar.copy, nc.scalar.copy)):
+            grouped = work.tile([P, PASSES, P, PACK], BF16, tag="x_grouped", name="x_grouped", align_bytes=64)
+            grouped_words = grouped[:].bitcast(F32)
+            for h in range(2):
+                copies[h](
+                    out=grouped_words[:, 2 * h : 2 * h + 2, :, :],
+                    in_=x_banks[m][h][:].rearrange("p (g u r) -> p g r u", g=2, u=2),
                 )
+            x_grouped[m] = grouped
+
+        def x_quantise(m):
             codes = keep.tile([P, PASSES, P], U32, name="x_codes%d" % m, align_bytes=64)
             scales = keep.tile([P, PASSES, P], U8, name="x_scales%d" % m, align_bytes=64)
             nc.vector.quantize_mx(
                 out=codes[:].rearrange("p g r -> p (g r)").bitcast(FP8X4),
                 scales=scales[:].rearrange("p g r -> p (g r)"),
-                in_=x_grouped[:].rearrange("p g r t -> p (g r t)"),
+                in_=x_grouped[m][:].rearrange("p g r t -> p (g r t)"),
             )
-            x_codes.append(codes)
-            x_scales.append(scales)
+            x_codes[m] = codes
+            x_scales[m] = scales
 
         rope_ps = fixed_banks.tile([P, TOK_TILES, ROPE], F32, name="rope_ps")
-        n_codes, n_scales = [], []
-        for m in range(TOK_TILES):
+        lat_banks, inv_rms_of, n_rows, n_banks, n_grouped, n_codes, n_scales = {}, {}, {}, {}, {}, {}, {}
+
+        def first_product(m):
             lat_ps = banks.tile([P, N_TILE], F32, tag="bank", name="lat_ps")
             for g in range(PASSES):
                 nc.tensor.matmul_mx(
                     out=lat_ps[:],
                     lhsT=x_codes[m][:, g, :].bitcast(FP8X4),
                     lhsT_scale=x_scales[m][:, g, :],
-                    rhs=w1_lat_codes[g][:].bitcast(FP8X4),
-                    rhs_scale=w1_lat_scales[g][:],
+                    rhs=w1_codes[g][:].bitcast(FP8X4),
+                    rhs_scale=w1_scales[g][:],
                     start=(g == 0),
                     stop=(g == PASSES - 1),
                 )
+            lat_banks[m] = lat_ps
+
+        def rope_product(m):
             for g in range(PASSES):
                 nc.tensor.matmul_mx(
                     out=rope_ps[:, m, :],
                     lhsT=x_codes[m][:, g, :].bitcast(FP8X4),
                     lhsT_scale=x_scales[m][:, g, :],
-                    rhs=w1_rope_codes[g][:].bitcast(FP8X4),
-                    rhs_scale=w1_rope_scales[g][:],
+                    rhs=rope_codes[:, g, :].bitcast(FP8X4),
+                    rhs_scale=rope_scales[:, g, :],
                     start=(g == 0),
                     stop=(g == PASSES - 1),
                 )
+
+        def norm_scalar(m):
             squares = work.tile([P, LORA], F32, tag="squares", name="squares")
             sum_sq = work.tile([P, 1], F32, tag="sum_sq", name="sum_sq")
-            nc.scalar.activation(out=squares[:], in_=lat_ps[:], func=ACT.Square, accum_out=sum_sq[:])
+            nc.scalar.activation(out=squares[:], in_=lat_banks[m][:], func=ACT.Square, accum_out=sum_sq[:])
             rms = work.tile([P, 1], F32, tag="rms", name="rms")
             nc.scalar.activation(out=rms[:], in_=sum_sq[:], func=ACT.Sqrt, scale=1.0 / LORA, bias=eps[:])
+            inv_rms_of[m] = rms
+
+        def norm_vector(m):
             inv_rms = work.tile([P, 1], F32, tag="inv_rms", name="inv_rms")
-            nc.vector.reciprocal(out=inv_rms[:], in_=rms[:])
+            nc.vector.reciprocal(out=inv_rms[:], in_=inv_rms_of[m][:])
             n_bf16 = work.tile([P, LORA], BF16, tag="n_bf16", name="n_bf16")
             nc.vector.scalar_tensor_tensor(
-                out=n_bf16[:], in0=lat_ps[:], scalar=inv_rms[:], in1=gain[:], op0=ALU.mult, op1=ALU.mult
+                out=n_bf16[:], in0=lat_banks[m][:], scalar=inv_rms[:], in1=gain[:], op0=ALU.mult, op1=ALU.mult
             )
-            n_t = fixed_banks.tile([P, PACK, P], BF16, name="n_t")
+            n_rows[m] = n_bf16
+
+        def n_transpose(m):
+            n_t = banks.tile([P, PACK, P], BF16, tag="bank", name="n_t")
             for t in range(PACK):
-                nc.tensor.transpose(n_t[:, t, :], n_bf16[:, t * P : (t + 1) * P], ident_bf16[:])
-            n_grouped = work.tile([P, P, PACK], BF16, tag="n_grouped", name="n_grouped", align_bytes=64)
-            nc.scalar.copy(out=n_grouped[:], in_=n_t[:].rearrange("p t r -> p r t"))
+                nc.tensor.transpose(n_t[:, t, :], n_rows[m][:, t * P : (t + 1) * P], ident_bf16[:])
+            n_banks[m] = n_t
+
+        def n_copy(m):
+            grouped = work.tile([P, P, PACK], BF16, tag="n_grouped", name="n_grouped", align_bytes=64)
+            nc.scalar.copy(out=grouped[:], in_=n_banks[m][:].rearrange("p t r -> p r t"))
+            n_grouped[m] = grouped
+
+        def n_quantise(m):
             codes = keep.tile([P, P], U32, name="n_codes%d" % m, align_bytes=64)
             scales = keep.tile([P, P], U8, name="n_scales%d" % m, align_bytes=64)
             nc.vector.quantize_mx(
-                out=codes[:].bitcast(FP8X4), scales=scales[:], in_=n_grouped[:].rearrange("p r t -> p (r t)")
+                out=codes[:].bitcast(FP8X4), scales=scales[:], in_=n_grouped[m][:].rearrange("p r t -> p (r t)")
             )
-            n_codes.append(codes)
-            n_scales.append(scales)
+            n_codes[m] = codes
+            n_scales[m] = scales
 
-        for c in range(W2_LOADS):
-            w2_codes, w2_scales = [], []
-            for h in range(HALVES):
-                cols = slice(h * N_TILE, (h + 1) * N_TILE)
-                w2_grouped = w2_work.tile([P, N_TILE, PACK], BF16, tag="w2_grouped", name="w2_grouped", align_bytes=64)
-                regroup(nc.vector.tensor_copy, w2_grouped[:], w2_raw[c][:, :, cols])
-                codes = keep.tile([P, N_TILE], U32, name="w2_codes%d_%d" % (c, h), align_bytes=64)
-                scales = keep.tile([P, N_TILE], U8, name="w2_scales%d_%d" % (c, h), align_bytes=64)
-                nc.vector.quantize_mx(
-                    out=codes[:].bitcast(FP8X4), scales=scales[:], in_=w2_grouped[:].rearrange("p c t -> p (c t)")
-                )
-                w2_codes.append(codes)
-                w2_scales.append(scales)
-            for m in range(TOK_TILES):
-                kv_sb = store.tile([P, W2_LOAD], F32, tag="kv_sb", name="kv_sb")
-                for h in range(HALVES):
-                    kv_ps = banks.tile([P, N_TILE], F32, tag="bank", name="kv_ps")
-                    nc.tensor.matmul_mx(
-                        out=kv_ps[:],
-                        lhsT=n_codes[m][:].bitcast(FP8X4),
-                        lhsT_scale=n_scales[m][:],
-                        rhs=w2_codes[h][:].bitcast(FP8X4),
-                        rhs_scale=w2_scales[h][:],
-                        start=True,
-                        stop=True,
-                    )
-                    nc.scalar.copy(out=kv_sb[:, h * N_TILE : (h + 1) * N_TILE], in_=kv_ps[:])
-                nc.sync.dma_start(
-                    out=kv_rows[m * P : (m + 1) * P, c * W2_LOAD : (c + 1) * W2_LOAD], in_=kv_sb[:]
-                )
+        w2_grouped, w2_codes, w2_scales = {}, {}, {}
+
+        def w2_regroup(i, copy):
+            grouped = work.tile([P, N_TILE, PACK], BF16, tag="w2_grouped", name="w2_grouped", align_bytes=64)
+            h = i % HALVES
+            regroup(copy, grouped[:], w2_raw[i // HALVES][:, :, h * N_TILE : (h + 1) * N_TILE])
+            w2_grouped[i] = grouped
+
+        def w2_quantise(i):
+            codes = keep.tile([P, N_TILE], U32, name="w2_codes%d" % i, align_bytes=64)
+            scales = keep.tile([P, N_TILE], U8, name="w2_scales%d" % i, align_bytes=64)
+            nc.vector.quantize_mx(
+                out=codes[:].bitcast(FP8X4), scales=scales[:], in_=w2_grouped[i][:].rearrange("p c t -> p (c t)")
+            )
+            w2_codes[i] = codes
+            w2_scales[i] = scales
+
+        kv_rows_sb = {}
+
+        def second_product(j, m, copy, whole_chunk):
+            h = j % HALVES if whole_chunk else 0
+            width = W2_LOAD if whole_chunk else N_TILE
+            if h == 0:
+                kv_rows_sb[m] = store.tile([P, width], F32, tag="kv_sb", name="kv_sb")
+            kv_ps = banks.tile([P, N_TILE], F32, tag="bank", name="kv_ps")
+            nc.tensor.matmul_mx(
+                out=kv_ps[:],
+                lhsT=n_codes[m][:].bitcast(FP8X4),
+                lhsT_scale=n_scales[m][:],
+                rhs=w2_codes[j][:].bitcast(FP8X4),
+                rhs_scale=w2_scales[j][:],
+                start=True,
+                stop=True,
+            )
+            copy(out=kv_rows_sb[m][:, h * N_TILE : (h + 1) * N_TILE], in_=kv_ps[:])
+            if (h + 1) * N_TILE == width:
+                last = (j + 1) * N_TILE
+                nc.sync.dma_start(out=kv_rows[m * P : (m + 1) * P, last - width : last], in_=kv_rows_sb[m][:])
 
         pairs = TOK_TILES * ROPE // 2
-        kr = rope_ps[:].rearrange("p m (i e) -> p (m i) e", e=2)
-        table = freq[:].rearrange("p m (i e) -> p (m i) e", e=2)
-        by_cos = keep.tile([P, pairs, 2], F32, name="by_cos")
-        by_sin = keep.tile([P, pairs, 2], F32, name="by_sin")
         rotated = keep.tile([P, pairs, 2], F32, name="rotated")
-        nc.vector.tensor_tensor(out=by_cos[:], in0=kr, in1=table[:, :, 0:1].to_broadcast([P, pairs, 2]), op=ALU.mult)
-        nc.vector.tensor_tensor(out=by_sin[:], in0=kr, in1=table[:, :, 1:2].to_broadcast([P, pairs, 2]), op=ALU.mult)
-        nc.vector.tensor_tensor(out=rotated[:, :, 0], in0=by_cos[:, :, 0], in1=by_sin[:, :, 1], op=ALU.subtract)
-        nc.vector.tensor_tensor(out=rotated[:, :, 1], in0=by_cos[:, :, 1], in1=by_sin[:, :, 0], op=ALU.add)
-        nc.sync.dma_start(
-            out=rope_rows.rearrange("(m p) f -> p m f", p=P),
-            in_=rotated[:].rearrange("p (m i) e -> p m (i e)", m=TOK_TILES),
-        )
+
+        def rotate():
+            kr = rope_ps[:].rearrange("p m (i e) -> p (m i) e", e=2)
+            table = freq[:].rearrange("p m (i e) -> p (m i) e", e=2)
+            by_cos = keep.tile([P, pairs, 2], F32, name="by_cos")
+            by_sin = keep.tile([P, pairs, 2], F32, name="by_sin")
+            nc.vector.tensor_tensor(out=by_cos[:], in0=kr, in1=table[:, :, 0:1].to_broadcast([P, pairs, 2]), op=ALU.mult)
+            nc.vector.tensor_tensor(out=by_sin[:], in0=kr, in1=table[:, :, 1:2].to_broadcast([P, pairs, 2]), op=ALU.mult)
+            nc.vector.tensor_tensor(out=rotated[:, :, 0], in0=by_cos[:, :, 0], in1=by_sin[:, :, 1], op=ALU.subtract)
+            nc.vector.tensor_tensor(out=rotated[:, :, 1], in0=by_cos[:, :, 1], in1=by_sin[:, :, 0], op=ALU.add)
+
+        def rope_store():
+            nc.sync.dma_start(
+                out=rope_rows.rearrange("(m p) f -> p m f", p=P),
+                in_=rotated[:].rearrange("p (m i) e -> p m (i e)", m=TOK_TILES),
+            )
+
+        S, V = nc.scalar.copy, nc.vector.tensor_copy
+        w1_regroup(0)
+        rope_regroup(0)
+        for g in range(1, PASSES):
+            w1_regroup(g)
+            w1_quantise(g - 1)
+        w1_quantise(3)
+        x_transpose(0)
+        x_copy(0)
+        for g in range(1, PASSES):
+            rope_regroup(g)
+        x_transpose(1)
+        x_copy(1)
+        x_quantise(0)
+        rope_quantise()
+        x_transpose(2)
+        x_copy(2)
+        first_product(0)
+        x_quantise(1)
+        x_transpose(3)
+        x_quantise(2)
+        norm_scalar(0)
+        x_copy(3)
+        first_product(1)
+        first_product(2)
+        norm_vector(0)
+        w2_regroup(0, V)
+        x_quantise(3)
+        norm_scalar(1)
+        n_transpose(0)
+        first_product(3)
+        norm_vector(1)
+        w2_quantise(0)
+        norm_scalar(2)
+        n_copy(0)
+        n_quantise(0)
+        n_transpose(1)
+        norm_vector(2)
+        w2_regroup(1, V)
+        norm_scalar(3)
+        n_copy(1)
+        second_product(0, 0, S, False)
+        n_transpose(2)
+        n_copy(2)
+        n_quantise(1)
+        norm_vector(3)
+        n_quantise(2)
+        w2_regroup(2, V)
+        second_product(0, 1, S, False)
+        n_transpose(3)
+        n_copy(3)
+        second_product(0, 2, S, False)
+        n_quantise(3)
+        w2_quantise(1)
+        second_product(0, 3, S, False)
+        for m in range(TOK_TILES):
+            rope_product(m)
+        w2_regroup(3, V)
+        w2_quantise(2)
+        for m in range(TOK_TILES):
+            second_product(1, m, S, False)
+        w2_regroup(4, V)
+        w2_quantise(3)
+        vset = {(3,3),(5,3),(7,1),(7,3)}
+        for c in range(1, W2_LOADS):
+            for i in range(HALVES * c + 3, min(PIECES, HALVES * c + 4) + 1):
+                if i < PIECES:
+                    w2_regroup(i, V)
+                w2_quantise(i - 1)
+            if c == 3:
+                rotate()
+            for m in range(TOK_TILES):
+                for h in range(HALVES):
+                    second_product(HALVES * c + h, m, V if (HALVES * c + h, m) in vset else S, False)
+                if c == W2_LOADS - 1 and m == 1:
+                    rope_store()

@@ -53,10 +53,9 @@ def tile_multiheadlatentattention_pa_kernel(tc, x, freq_cis, Wckv, kv_norm_w, Wd
         store = ctx.enter_context(tc.tile_pool(name="store", bufs=8))
         banks = ctx.enter_context(tc.psum_pool(name="banks", bufs=7))
         fixed_banks = ctx.enter_context(tc.psum_pool(name="fixed_banks", bufs=1))
-        ctx.enter_context(tc.manual_schedule())
 
         gain_row = keep.tile([P, LORA], BF16, name="gain_row")
-        nc.gpsimd.memset(gain_row[:], 0.0)
+        nc.vector.memset(gain_row[:], 0.0)
         ident_f32 = keep.tile([P, P], F32, name="ident_f32")
         make_identity(nc, ident_f32[:])
         ident_bf16 = keep.tile([P, P], BF16, name="ident_bf16")
@@ -68,7 +67,7 @@ def tile_multiheadlatentattention_pa_kernel(tc, x, freq_cis, Wckv, kv_norm_w, Wd
         warm = keep.tile([P, 1], F32, name="warm")
         nc.scalar.activation(out=warm[:], in_=eps[:], func=ACT.Sqrt)
 
-        nc.sync.dma_start(out=gain_row[0:1, :], in_=kv_norm_w.rearrange("(o n) -> o n", o=1))
+        nc.scalar.dma_start(out=gain_row[0:1, :], in_=kv_norm_w.rearrange("(o n) -> o n", o=1))
 
         w1_raw, x_raw, w2_raw = {}, {}, {}
 
@@ -108,10 +107,12 @@ def tile_multiheadlatentattention_pa_kernel(tc, x, freq_cis, Wckv, kv_norm_w, Wd
         freq = keep.tile([P, TOK_TILES, ROPE], BF16, name="freq")
         nc.sync.dma_start(out=freq[:], in_=freq_cis.rearrange("(m p) i e -> p m (i e)", p=P))
 
-        gain_ps = banks.tile([P, N_TILE], F32, tag="bank", name="gain_ps")
-        nc.tensor.matmul(out=gain_ps[:], lhsT=ones[:], rhs=gain_row[:], start=True, stop=True)
         gain = keep.tile([P, LORA], F32, name="gain")
-        nc.scalar.copy(out=gain[:], in_=gain_ps[:])
+
+        def spread_gain():
+            gain_ps = banks.tile([P, N_TILE], F32, tag="bank", name="gain_ps")
+            nc.tensor.matmul(out=gain_ps[:], lhsT=ones[:], rhs=gain_row[:], start=True, stop=True)
+            nc.scalar.copy(out=gain[:], in_=gain_ps[:])
 
         w1_grouped, w1_codes, w1_scales = {}, {}, {}
         rope_grouped = keep.tile([P, PASSES, ROPE, PACK], BF16, name="rope_grouped", align_bytes=64)
@@ -317,6 +318,7 @@ def tile_multiheadlatentattention_pa_kernel(tc, x, freq_cis, Wckv, kv_norm_w, Wd
         rope_quantise()
         x_transpose(2)
         x_copy(2)
+        spread_gain()
         first_product(0)
         x_quantise(1)
         x_transpose(3)
@@ -341,26 +343,26 @@ def tile_multiheadlatentattention_pa_kernel(tc, x, freq_cis, Wckv, kv_norm_w, Wd
         w2_regroup(1, V)
         norm_scalar(3)
         n_copy(1)
-        second_product(0, 0, S, False)
+        second_product(0, 0, S, True)
         n_transpose(2)
         n_copy(2)
         n_quantise(1)
         norm_vector(3)
         n_quantise(2)
         w2_regroup(2, V)
-        second_product(0, 1, S, False)
+        second_product(0, 1, S, True)
         n_transpose(3)
         n_copy(3)
-        second_product(0, 2, S, False)
+        second_product(0, 2, S, True)
         n_quantise(3)
         w2_quantise(1)
-        second_product(0, 3, S, False)
+        second_product(0, 3, S, True)
         for m in range(TOK_TILES):
             rope_product(m)
         w2_regroup(3, V)
         w2_quantise(2)
         for m in range(TOK_TILES):
-            second_product(1, m, S, False)
+            second_product(1, m, S, True)
         w2_regroup(4, V)
         w2_quantise(3)
         vset = {(3,3),(5,3),(7,1),(7,3)}
@@ -373,6 +375,6 @@ def tile_multiheadlatentattention_pa_kernel(tc, x, freq_cis, Wckv, kv_norm_w, Wd
                 rotate()
             for m in range(TOK_TILES):
                 for h in range(HALVES):
-                    second_product(HALVES * c + h, m, V if (HALVES * c + h, m) in vset else S, False)
+                    second_product(HALVES * c + h, m, V if (HALVES * c + h, m) in vset else S, True)
                 if c == W2_LOADS - 1 and m == 1:
                     rope_store()

@@ -335,15 +335,17 @@ def tile_multiheadlatentattention_pa_kernel(tc, x, freq_cis, Wckv, kv_norm_w, Wd
         first_product(3)
         norm_vector(1)
         w2_quantise(0)
+        w2_regroup(1, V)
         norm_scalar(2)
         n_copy(0)
         n_quantise(0)
         n_transpose(1)
         norm_vector(2)
-        w2_regroup(1, V)
+        w2_quantise(1)
         norm_scalar(3)
         n_copy(1)
         second_product(0, 0, S, True)
+        second_product(1, 0, S, True)
         n_transpose(2)
         n_copy(2)
         n_quantise(1)
@@ -351,18 +353,18 @@ def tile_multiheadlatentattention_pa_kernel(tc, x, freq_cis, Wckv, kv_norm_w, Wd
         n_quantise(2)
         w2_regroup(2, V)
         second_product(0, 1, S, True)
+        second_product(1, 1, S, True)
         n_transpose(3)
         n_copy(3)
         second_product(0, 2, S, True)
+        second_product(1, 2, S, True)
         n_quantise(3)
-        w2_quantise(1)
         second_product(0, 3, S, True)
+        second_product(1, 3, S, True)
         for m in range(TOK_TILES):
             rope_product(m)
         w2_regroup(3, V)
         w2_quantise(2)
-        for m in range(TOK_TILES):
-            second_product(1, m, S, True)
         w2_regroup(4, V)
         w2_quantise(3)
         vset = {(3,3),(5,3),(7,1),(7,3)}

@@ -65,7 +65,7 @@ def tile_multiheadlatentattention_pa_kernel(tc, x, freq_cis, Wckv, kv_norm_w, Wd
         eps = keep.tile([P, 1], F32, name="eps")
         nc.vector.memset(eps[:], EPS)
         warm = keep.tile([P, 1], F32, name="warm")
-        nc.scalar.activation(out=warm[:], in_=eps[:], func=ACT.Sqrt)
+        nc.scalar.activation(out=warm[:], in_=eps[:], func=ACT.Abs_reciprocal_sqrt)
 
         nc.scalar.dma_start(out=gain_row[0:1, :], in_=kv_norm_w.rearrange("(o n) -> o n", o=1))
 
@@ -210,23 +210,25 @@ def tile_multiheadlatentattention_pa_kernel(tc, x, freq_cis, Wckv, kv_norm_w, Wd
             squares = work.tile([P, LORA], F32, tag="squares", name="squares")
             sum_sq = work.tile([P, 1], F32, tag="sum_sq", name="sum_sq")
             nc.scalar.activation(out=squares[:], in_=lat_banks[m][:], func=ACT.Square, accum_out=sum_sq[:])
-            rms = work.tile([P, 1], F32, tag="rms", name="rms")
-            nc.scalar.activation(out=rms[:], in_=sum_sq[:], func=ACT.Sqrt, scale=1.0 / LORA, bias=eps[:])
-            inv_rms_of[m] = rms
+            inv_rms = work.tile([P, 1], F32, tag="inv_rms", name="inv_rms")
+            nc.scalar.activation(
+                out=inv_rms[:], in_=sum_sq[:], func=ACT.Abs_reciprocal_sqrt, scale=1.0 / LORA, bias=eps[:]
+            )
+            inv_rms_of[m] = inv_rms
 
         def norm_vector(m):
-            inv_rms = work.tile([P, 1], F32, tag="inv_rms", name="inv_rms")
-            nc.vector.reciprocal(out=inv_rms[:], in_=inv_rms_of[m][:])
             n_bf16 = work.tile([P, LORA], BF16, tag="n_bf16", name="n_bf16")
             nc.vector.scalar_tensor_tensor(
-                out=n_bf16[:], in0=lat_banks[m][:], scalar=inv_rms[:], in1=gain[:], op0=ALU.mult, op1=ALU.mult
+                out=n_bf16[:], in0=lat_banks[m][:], scalar=inv_rms_of[m][:], in1=gain[:], op0=ALU.mult, op1=ALU.mult
             )
             n_rows[m] = n_bf16
 
         def n_transpose(m):
             n_t = banks.tile([P, PACK, P], BF16, tag="bank", name="n_t")
             for t in range(PACK):
-                nc.tensor.transpose(n_t[:, t, :], n_rows[m][:, t * P : (t + 1) * P], ident_bf16[:])
+                nc.tensor.matmul(
+                    out=n_t[:, t, :], lhsT=n_rows[m][:, t * P : (t + 1) * P], rhs=ident_bf16[:], start=True, stop=True
+                )
             n_banks[m] = n_t
 
         def n_copy(m):
@@ -302,81 +304,66 @@ def tile_multiheadlatentattention_pa_kernel(tc, x, freq_cis, Wckv, kv_norm_w, Wd
             )
 
         S, V = nc.scalar.copy, nc.vector.tensor_copy
-        w1_regroup(0)
-        rope_regroup(0)
-        for g in range(1, PASSES):
+
+        def tile_at(m):
+            return 0 <= m < TOK_TILES
+
+        def w2_prepare(tick):
+            c, phase = divmod(tick, 3)
+            if 0 <= c < W2_LOADS:
+                if phase == 0:
+                    w2_regroup(HALVES * c, V)
+                if phase == 1:
+                    w2_quantise(HALVES * c)
+                    w2_regroup(HALVES * c + 1, V)
+                if phase == 2:
+                    w2_quantise(HALVES * c + 1)
+
+        for g in range(PASSES):
             w1_regroup(g)
-            w1_quantise(g - 1)
-        w1_quantise(3)
-        x_transpose(0)
-        x_copy(0)
-        for g in range(1, PASSES):
-            rope_regroup(g)
-        x_transpose(1)
-        x_copy(1)
-        x_quantise(0)
-        rope_quantise()
-        x_transpose(2)
-        x_copy(2)
-        spread_gain()
-        first_product(0)
-        x_quantise(1)
-        x_transpose(3)
-        x_quantise(2)
-        norm_scalar(0)
-        x_copy(3)
-        first_product(1)
-        first_product(2)
-        norm_vector(0)
-        w2_regroup(0, V)
-        x_quantise(3)
-        norm_scalar(1)
-        n_transpose(0)
-        first_product(3)
-        norm_vector(1)
-        w2_quantise(0)
-        w2_regroup(1, V)
-        norm_scalar(2)
-        n_copy(0)
-        n_quantise(0)
-        n_transpose(1)
-        norm_vector(2)
-        w2_quantise(1)
-        norm_scalar(3)
-        n_copy(1)
-        second_product(0, 0, S, True)
-        second_product(1, 0, S, True)
-        n_transpose(2)
-        n_copy(2)
-        n_quantise(1)
-        norm_vector(3)
-        n_quantise(2)
-        w2_regroup(2, V)
-        second_product(0, 1, S, True)
-        second_product(1, 1, S, True)
-        n_transpose(3)
-        n_copy(3)
-        second_product(0, 2, S, True)
-        second_product(1, 2, S, True)
-        n_quantise(3)
-        second_product(0, 3, S, True)
-        second_product(1, 3, S, True)
+            if g > 0:
+                w1_quantise(g - 1)
+        w1_quantise(PASSES - 1)
+
+        STEPS = TOK_TILES + 6
+        for k in range(STEPS):
+            if tile_at(k):
+                x_transpose(k)
+            if tile_at(k - 3):
+                norm_scalar(k - 3)
+            if tile_at(k):
+                x_copy(k)
+            if k == 0:
+                for g in range(PASSES):
+                    rope_regroup(g)
+            if tile_at(k - 1):
+                x_quantise(k - 1)
+            if k == 1:
+                rope_quantise()
+            if k == 2:
+                spread_gain()
+            if tile_at(k - 2):
+                first_product(k - 2)
+            if tile_at(k - 5):
+                n_copy(k - 5)
+                n_quantise(k - 5)
+            if tile_at(k - 6):
+                for h in range(HALVES):
+                    second_product(h, k - 6, S, True)
+            if tile_at(k - 4):
+                n_transpose(k - 4)
+            if tile_at(k - 3):
+                norm_vector(k - 3)
+            w2_prepare(k - 3)
         for m in range(TOK_TILES):
             rope_product(m)
-        w2_regroup(3, V)
-        w2_quantise(2)
-        w2_regroup(4, V)
-        w2_quantise(3)
-        vset = {(3,3),(5,3),(7,1),(7,3)}
         for c in range(1, W2_LOADS):
-            for i in range(HALVES * c + 3, min(PIECES, HALVES * c + 4) + 1):
-                if i < PIECES:
-                    w2_regroup(i, V)
-                w2_quantise(i - 1)
-            if c == 3:
+            if c == W2_LOADS - 1:
                 rotate()
             for m in range(TOK_TILES):
+                w2_prepare(STEPS - 3 + TOK_TILES * (c - 1) + m)
                 for h in range(HALVES):
-                    second_product(HALVES * c + h, m, V if (HALVES * c + h, m) in vset else S, True)
+                    by_vector = h == 1 and m > 0 and c >= 2
+                    second_product(HALVES * c + h, m, V if by_vector else S, True)
                 if c == W2_LOADS - 1 and m == 1:
                     rope_store()

@@ -58,8 +58,6 @@ def tile_multiheadlatentattention_pa_kernel(tc, x, freq_cis, Wckv, kv_norm_w, Wd
         nc.vector.memset(gain_row[:], 0.0)
         ident_f32 = keep.tile([P, P], F32, name="ident_f32")
         make_identity(nc, ident_f32[:])
-        ident_bf16 = keep.tile([P, P], BF16, name="ident_bf16")
-        make_identity(nc, ident_bf16[:])
         ones = keep.tile([P, P], BF16, name="ones")
         nc.vector.memset(ones[:], 1.0)
         eps = keep.tile([P, 1], F32, name="eps")
@@ -88,7 +86,7 @@ def tile_multiheadlatentattention_pa_kernel(tc, x, freq_cis, Wckv, kv_norm_w, Wd
             raw = keep.tile([P, PACK, W2_LOAD], BF16, name="w2_raw%d" % c)
             nc.sync.dma_start(
                 out=raw[:],
-                in_=Wdkv[:, c * W2_LOAD : (c + 1) * W2_LOAD].rearrange("(t p) n -> p t n", p=P),
+                in_=Wdkv[:, c * W2_LOAD : (c + 1) * W2_LOAD].rearrange("(p t) n -> p t n", p=P),
             )
             w2_raw[c] = raw
 
@@ -224,16 +222,15 @@ def tile_multiheadlatentattention_pa_kernel(tc, x, freq_cis, Wckv, kv_norm_w, Wd
             n_rows[m] = n_bf16
 
         def n_transpose(m):
-            n_t = banks.tile([P, PACK, P], BF16, tag="bank", name="n_t")
-            for t in range(PACK):
-                nc.tensor.matmul(
-                    out=n_t[:, t, :], lhsT=n_rows[m][:, t * P : (t + 1) * P], rhs=ident_bf16[:], start=True, stop=True
-                )
+            n_words = n_rows[m][:].bitcast(F32)
+            n_t = banks.tile([P, 2, P], F32, tag="bank", name="n_t")
+            for u in range(2):
+                nc.tensor.transpose(n_t[:, u, :], n_words[:, u : LORA // 2 : 2], ident_f32[:])
             n_banks[m] = n_t
 
         def n_copy(m):
             grouped = work.tile([P, P, PACK], BF16, tag="n_grouped", name="n_grouped", align_bytes=64)
-            nc.scalar.copy(out=grouped[:], in_=n_banks[m][:].rearrange("p t r -> p r t"))
+            nc.scalar.copy(out=grouped[:].bitcast(F32), in_=n_banks[m][:].rearrange("p u r -> p r u"))
             n_grouped[m] = grouped
 
         def n_quantise(m):

@@ -82,13 +82,11 @@ def tile_multiheadlatentattention_pa_kernel(tc, x, freq_cis, Wckv, kv_norm_w, Wd
             nc.sync.dma_start(out=raw[:], in_=x_rows[m * P : (m + 1) * P, :])
             x_raw[m] = raw
 
-        def load_w2(c):
-            raw = keep.tile([P, PACK, W2_LOAD], BF16, name="w2_raw%d" % c)
-            nc.sync.dma_start(
-                out=raw[:],
-                in_=Wdkv[:, c * W2_LOAD : (c + 1) * W2_LOAD].rearrange("(p t) n -> p t n", p=P),
-            )
-            w2_raw[c] = raw
+        def load_w2(first, width):
+            raw = keep.tile([P, PACK, width], BF16, name="w2_raw%d" % first)
+            nc.sync.dma_start(out=raw[:], in_=Wdkv[:, first : first + width].rearrange("(p t) n -> p t n", p=P))
+            for offset in range(0, width, N_TILE):
+                w2_raw[(first + offset) // N_TILE] = raw[:, :, offset : offset + N_TILE]
 
         load_w1(0)
         load_w1(1)
@@ -97,11 +95,11 @@ def tile_multiheadlatentattention_pa_kernel(tc, x, freq_cis, Wckv, kv_norm_w, Wd
         load_x(0)
         load_x(1)
         load_x(2)
+        load_w2(0, N_TILE)
         load_x(3)
-        load_w2(0)
-        load_w2(1)
-        load_w2(2)
-        load_w2(3)
+        load_w2(N_TILE, N_TILE)
+        for c in range(1, W2_LOADS):
+            load_w2(c * W2_LOAD, W2_LOAD)
         freq = keep.tile([P, TOK_TILES, ROPE], BF16, name="freq")
         nc.sync.dma_start(out=freq[:], in_=freq_cis.rearrange("(m p) i e -> p m (i e)", p=P))
 
@@ -246,8 +244,7 @@ def tile_multiheadlatentattention_pa_kernel(tc, x, freq_cis, Wckv, kv_norm_w, Wd
 
         def w2_regroup(i, copy):
             grouped = work.tile([P, N_TILE, PACK], BF16, tag="w2_grouped", name="w2_grouped", align_bytes=64)
-            h = i % HALVES
-            regroup(copy, grouped[:], w2_raw[i // HALVES][:, :, h * N_TILE : (h + 1) * N_TILE])
+            regroup(copy, grouped[:], w2_raw[i])
             w2_grouped[i] = grouped
 
         def w2_quantise(i):

from contextlib import ExitStack

import concourse.mybir as mybir
from concourse.masks import make_identity

F32 = mybir.dt.float32
BF16 = mybir.dt.bfloat16
U32 = mybir.dt.uint32
U8 = mybir.dt.uint8
FP8X4 = mybir.dt.float8_e4m3fn_x4
ACT = mybir.ActivationFunctionType
ALU = mybir.AluOpType

P = 128
PACK = 4
K_PASS = P * PACK

T = 512
C = 2048
LORA = 512
ROPE = 128
KVW = 4096
EPS = 1e-6

TOK_TILES = T // P
PASSES = C // K_PASS
N_TILE = 512
W2_LOAD = 1024
W2_LOADS = KVW // W2_LOAD
HALVES = W2_LOAD // N_TILE
PIECES = KVW // N_TILE
W1_VECTOR_COLS = 256

FLOPS = 2 * T * C * (LORA + ROPE) + 2 * T * LORA * KVW


def regroup(copy, grouped, raw):
    copy(
        out=grouped.rearrange("p (c i) t -> p c t i", i=4),
        in_=raw.rearrange("p t (c i) -> p c t i", i=4),
    )


def tile_multiheadlatentattention_pa_kernel(tc, x, freq_cis, Wckv, kv_norm_w, Wdkv, out_0, out_1):
    nc = tc.nc
    x_rows = x.flatten_outer_dims()
    kv_rows = out_0.flatten_outer_dims()
    rope_rows = out_1.flatten_outer_dims()

    with ExitStack() as ctx:
        keep = ctx.enter_context(tc.tile_pool(name="keep", bufs=1))
        work = ctx.enter_context(tc.tile_pool(name="work", bufs=3))
        store = ctx.enter_context(tc.tile_pool(name="store", bufs=8))
        banks = ctx.enter_context(tc.psum_pool(name="banks", bufs=7))
        fixed_banks = ctx.enter_context(tc.psum_pool(name="fixed_banks", bufs=1))

        gain_row = keep.tile([P, LORA], BF16, name="gain_row")
        nc.vector.memset(gain_row[:], 0.0)
        ident_f32 = keep.tile([P, P], F32, name="ident_f32")
        make_identity(nc, ident_f32[:])
        ones = keep.tile([P, P], BF16, name="ones")
        nc.vector.memset(ones[:], 1.0)
        eps = keep.tile([P, 1], F32, name="eps")
        nc.vector.memset(eps[:], EPS)
        warm = keep.tile([P, 1], F32, name="warm")
        nc.scalar.activation(out=warm[:], in_=eps[:], func=ACT.Abs_reciprocal_sqrt)

        nc.scalar.dma_start(out=gain_row[0:1, :], in_=kv_norm_w.rearrange("(o n) -> o n", o=1))

        w1_raw, x_raw, w2_raw = {}, {}, {}

        def load_w1(g):
            raw = keep.tile([P, PACK, LORA + ROPE], BF16, name="w1_raw%d" % g)
            nc.sync.dma_start(
                out=raw[:].rearrange("q (u e) c -> q u (e c)", u=2),
                in_=Wckv[g * K_PASS : (g + 1) * K_PASS, :].rearrange("(u q e) c -> q u (e c)", u=2, e=2),
            )
            w1_raw[g] = raw

        def load_x(m):
            raw = keep.tile([P, C], BF16, name="x_raw%d" % m)
            nc.sync.dma_start(out=raw[:], in_=x_rows[m * P : (m + 1) * P, :])
            x_raw[m] = raw

        def load_w2(first, width):
            raw = keep.tile([P, PACK, width], BF16, name="w2_raw%d" % first)
            nc.sync.dma_start(out=raw[:], in_=Wdkv[:, first : first + width].rearrange("(p t) n -> p t n", p=P))
            for offset in range(0, width, N_TILE):
                w2_raw[(first + offset) // N_TILE] = raw[:, :, offset : offset + N_TILE]

        load_w1(0)
        load_w1(1)
        load_w1(2)
        load_w1(3)
        load_x(0)
        load_x(1)
        load_x(2)
        load_w2(0, N_TILE)
        load_x(3)
        load_w2(N_TILE, N_TILE)
        for c in range(1, W2_LOADS):
            load_w2(c * W2_LOAD, W2_LOAD)
        freq = keep.tile([P, TOK_TILES, ROPE], BF16, name="freq")
        nc.sync.dma_start(out=freq[:], in_=freq_cis.rearrange("(m p) i e -> p m (i e)", p=P))

        gain = keep.tile([P, LORA], F32, name="gain")

        def spread_gain():
            gain_ps = banks.tile([P, N_TILE], F32, tag="bank", name="gain_ps")
            nc.tensor.matmul(out=gain_ps[:], lhsT=ones[:], rhs=gain_row[:], start=True, stop=True)
            nc.scalar.copy(out=gain[:], in_=gain_ps[:])

        w1_grouped, w1_codes, w1_scales = {}, {}, {}
        rope_grouped = keep.tile([P, PASSES, ROPE, PACK], BF16, name="rope_grouped", align_bytes=64)
        rope_codes = keep.tile([P, PASSES, ROPE], U32, name="rope_codes", align_bytes=64)
        rope_scales = keep.tile([P, PASSES, ROPE], U8, name="rope_scales", align_bytes=64)

        def w1_regroup(g):
            grouped = work.tile([P, LORA, PACK], BF16, tag="w1_grouped", name="w1_grouped", align_bytes=64)
            regroup(nc.vector.tensor_copy, grouped[:, 0:W1_VECTOR_COLS, :], w1_raw[g][:, :, 0:W1_VECTOR_COLS])
            regroup(nc.scalar.copy, grouped[:, W1_VECTOR_COLS:LORA, :], w1_raw[g][:, :, W1_VECTOR_COLS:LORA])
            w1_grouped[g] = grouped

        def rope_regroup(g):
            regroup(nc.vector.tensor_copy, rope_grouped[:, g, :, :], w1_raw[g][:, :, LORA : LORA + ROPE])

        def w1_quantise(g):
            codes = keep.tile([P, LORA], U32, name="w1_codes%d" % g, align_bytes=64)
            scales = keep.tile([P, LORA], U8, name="w1_scales%d" % g, align_bytes=64)
            nc.vector.quantize_mx(
                out=codes[:].bitcast(FP8X4), scales=scales[:], in_=w1_grouped[g][:].rearrange("p c t -> p (c t)")
            )
            w1_codes[g] = codes
            w1_scales[g] = scales

        def rope_quantise():
            nc.vector.quantize_mx(
                out=rope_codes[:].rearrange("p g c -> p (g c)").bitcast(FP8X4),
                scales=rope_scales[:].rearrange("p g c -> p (g c)"),
                in_=rope_grouped[:].rearrange("p g c t -> p (g c t)"),
            )

        x_banks, x_grouped, x_codes, x_scales = {}, {}, {}, {}

        def x_transpose(m):
            x_words = x_raw[m][:].bitcast(F32)
            x_banks[m] = []
            for h in range(2):
                xt = banks.tile([P, N_TILE], F32, tag="bank", name="xt")
                for s in range(4):
                    w0 = (4 * h + s) * P
                    nc.tensor.transpose(xt[:, s * P : (s + 1) * P], x_words[:, w0 : w0 + P], ident_f32[:])
                x_banks[m].append(xt)

        def x_copy(m, copies=(nc.scalar.copy, nc.scalar.copy)):
            grouped = work.tile([P, PASSES, P, PACK], BF16, tag="x_grouped", name="x_grouped", align_bytes=64)
            grouped_words = grouped[:].bitcast(F32)
            for h in range(2):
                copies[h](
                    out=grouped_words[:, 2 * h : 2 * h + 2, :, :],
                    in_=x_banks[m][h][:].rearrange("p (g u r) -> p g r u", g=2, u=2),
                )
            x_grouped[m] = grouped

        def x_quantise(m):
            codes = keep.tile([P, PASSES, P], U32, name="x_codes%d" % m, align_bytes=64)
            scales = keep.tile([P, PASSES, P], U8, name="x_scales%d" % m, align_bytes=64)
            nc.vector.quantize_mx(
                out=codes[:].rearrange("p g r -> p (g r)").bitcast(FP8X4),
                scales=scales[:].rearrange("p g r -> p (g r)"),
                in_=x_grouped[m][:].rearrange("p g r t -> p (g r t)"),
            )
            x_codes[m] = codes
            x_scales[m] = scales

        rope_ps = fixed_banks.tile([P, TOK_TILES, ROPE], F32, name="rope_ps")
        lat_banks, inv_rms_of, n_rows, n_banks, n_grouped, n_codes, n_scales = {}, {}, {}, {}, {}, {}, {}

        def first_product(m):
            lat_ps = banks.tile([P, N_TILE], F32, tag="bank", name="lat_ps")
            for g in range(PASSES):
                nc.tensor.matmul_mx(
                    out=lat_ps[:],
                    lhsT=x_codes[m][:, g, :].bitcast(FP8X4),
                    lhsT_scale=x_scales[m][:, g, :],
                    rhs=w1_codes[g][:].bitcast(FP8X4),
                    rhs_scale=w1_scales[g][:],
                    start=(g == 0),
                    stop=(g == PASSES - 1),
                )
            lat_banks[m] = lat_ps

        def rope_product(m):
            for g in range(PASSES):
                nc.tensor.matmul_mx(
                    out=rope_ps[:, m, :],
                    lhsT=x_codes[m][:, g, :].bitcast(FP8X4),
                    lhsT_scale=x_scales[m][:, g, :],
                    rhs=rope_codes[:, g, :].bitcast(FP8X4),
                    rhs_scale=rope_scales[:, g, :],
                    start=(g == 0),
                    stop=(g == PASSES - 1),
                )

        def norm_scalar(m):
            squares = work.tile([P, LORA], F32, tag="squares", name="squares")
            sum_sq = work.tile([P, 1], F32, tag="sum_sq", name="sum_sq")
            nc.scalar.activation(out=squares[:], in_=lat_banks[m][:], func=ACT.Square, accum_out=sum_sq[:])
            inv_rms = work.tile([P, 1], F32, tag="inv_rms", name="inv_rms")
            nc.scalar.activation(
                out=inv_rms[:], in_=sum_sq[:], func=ACT.Abs_reciprocal_sqrt, scale=1.0 / LORA, bias=eps[:]
            )
            inv_rms_of[m] = inv_rms

        def norm_vector(m):
            n_bf16 = work.tile([P, LORA], BF16, tag="n_bf16", name="n_bf16")
            nc.vector.scalar_tensor_tensor(
                out=n_bf16[:], in0=lat_banks[m][:], scalar=inv_rms_of[m][:], in1=gain[:], op0=ALU.mult, op1=ALU.mult
            )
            n_rows[m] = n_bf16

        def n_transpose(m):
            n_words = n_rows[m][:].bitcast(F32)
            n_t = banks.tile([P, 2, P], F32, tag="bank", name="n_t")
            for u in range(2):
                nc.tensor.transpose(n_t[:, u, :], n_words[:, u : LORA // 2 : 2], ident_f32[:])
            n_banks[m] = n_t

        def n_copy(m):
            grouped = work.tile([P, P, PACK], BF16, tag="n_grouped", name="n_grouped", align_bytes=64)
            nc.scalar.copy(out=grouped[:].bitcast(F32), in_=n_banks[m][:].rearrange("p u r -> p r u"))
            n_grouped[m] = grouped

        def n_quantise(m):
            codes = keep.tile([P, P], U32, name="n_codes%d" % m, align_bytes=64)
            scales = keep.tile([P, P], U8, name="n_scales%d" % m, align_bytes=64)
            nc.vector.quantize_mx(
                out=codes[:].bitcast(FP8X4), scales=scales[:], in_=n_grouped[m][:].rearrange("p r t -> p (r t)")
            )
            n_codes[m] = codes
            n_scales[m] = scales

        w2_grouped, w2_codes, w2_scales = {}, {}, {}

        def w2_regroup(i, copy):
            grouped = work.tile([P, N_TILE, PACK], BF16, tag="w2_grouped", name="w2_grouped", align_bytes=64)
            regroup(copy, grouped[:], w2_raw[i])
            w2_grouped[i] = grouped

        def w2_quantise(i):
            codes = keep.tile([P, N_TILE], U32, name="w2_codes%d" % i, align_bytes=64)
            scales = keep.tile([P, N_TILE], U8, name="w2_scales%d" % i, align_bytes=64)
            nc.vector.quantize_mx(
                out=codes[:].bitcast(FP8X4), scales=scales[:], in_=w2_grouped[i][:].rearrange("p c t -> p (c t)")
            )
            w2_codes[i] = codes
            w2_scales[i] = scales

        kv_rows_sb = {}

        def second_product(j, m, copy, whole_chunk):
            h = j % HALVES if whole_chunk else 0
            width = W2_LOAD if whole_chunk else N_TILE
            if h == 0:
                kv_rows_sb[m] = store.tile([P, width], F32, tag="kv_sb", name="kv_sb")
            kv_ps = banks.tile([P, N_TILE], F32, tag="bank", name="kv_ps")
            nc.tensor.matmul_mx(
                out=kv_ps[:],
                lhsT=n_codes[m][:].bitcast(FP8X4),
                lhsT_scale=n_scales[m][:],
                rhs=w2_codes[j][:].bitcast(FP8X4),
                rhs_scale=w2_scales[j][:],
                start=True,
                stop=True,
            )
            copy(out=kv_rows_sb[m][:, h * N_TILE : (h + 1) * N_TILE], in_=kv_ps[:])
            if (h + 1) * N_TILE == width:
                last = (j + 1) * N_TILE
                nc.sync.dma_start(out=kv_rows[m * P : (m + 1) * P, last - width : last], in_=kv_rows_sb[m][:])

        pairs = TOK_TILES * ROPE // 2
        rotated = keep.tile([P, pairs, 2], F32, name="rotated")

        def rotate():
            kr = rope_ps[:].rearrange("p m (i e) -> p (m i) e", e=2)
            table = freq[:].rearrange("p m (i e) -> p (m i) e", e=2)
            by_cos = keep.tile([P, pairs, 2], F32, name="by_cos")
            by_sin = keep.tile([P, pairs, 2], F32, name="by_sin")
            nc.vector.tensor_tensor(out=by_cos[:], in0=kr, in1=table[:, :, 0:1].to_broadcast([P, pairs, 2]), op=ALU.mult)
            nc.vector.tensor_tensor(out=by_sin[:], in0=kr, in1=table[:, :, 1:2].to_broadcast([P, pairs, 2]), op=ALU.mult)
            nc.vector.tensor_tensor(out=rotated[:, :, 0], in0=by_cos[:, :, 0], in1=by_sin[:, :, 1], op=ALU.subtract)
            nc.vector.tensor_tensor(out=rotated[:, :, 1], in0=by_cos[:, :, 1], in1=by_sin[:, :, 0], op=ALU.add)

        def rope_store():
            nc.sync.dma_start(
                out=rope_rows.rearrange("(m p) f -> p m f", p=P),
                in_=rotated[:].rearrange("p (m i) e -> p m (i e)", m=TOK_TILES),
            )

        S, V = nc.scalar.copy, nc.vector.tensor_copy

        def tile_at(m):
            return 0 <= m < TOK_TILES

        def w2_prepare(tick):
            c, phase = divmod(tick, 3)
            if 0 <= c < W2_LOADS:
                if phase == 0:
                    w2_regroup(HALVES * c, V)
                if phase == 1:
                    w2_quantise(HALVES * c)
                    w2_regroup(HALVES * c + 1, V)
                if phase == 2:
                    w2_quantise(HALVES * c + 1)

        for g in range(PASSES):
            w1_regroup(g)
            if g > 0:
                w1_quantise(g - 1)
        w1_quantise(PASSES - 1)

        STEPS = TOK_TILES + 6
        for k in range(STEPS):
            if tile_at(k):
                x_transpose(k)
            if tile_at(k - 3):
                norm_scalar(k - 3)
            if tile_at(k):
                x_copy(k)
            if k == 0:
                for g in range(PASSES):
                    rope_regroup(g)
            if tile_at(k - 1):
                x_quantise(k - 1)
            if k == 1:
                rope_quantise()
            if k == 2:
                spread_gain()
            if tile_at(k - 2):
                first_product(k - 2)
            if tile_at(k - 5):
                n_copy(k - 5)
                n_quantise(k - 5)
            if tile_at(k - 6):
                for h in range(HALVES):
                    second_product(h, k - 6, S, True)
            if tile_at(k - 4):
                n_transpose(k - 4)
            if tile_at(k - 3):
                norm_vector(k - 3)
            w2_prepare(k - 3)
        for m in range(TOK_TILES):
            rope_product(m)
        for c in range(1, W2_LOADS):
            if c == W2_LOADS - 1:
                rotate()
            for m in range(TOK_TILES):
                w2_prepare(STEPS - 3 + TOK_TILES * (c - 1) + m)
                for h in range(HALVES):
                    by_vector = h == 1 and m > 0 and c >= 2
                    second_product(HALVES * c + h, m, V if by_vector else S, True)
                if c == W2_LOADS - 1 and m == 1:
                    rope_store()
